import numpy as np
import ml_dtypes


def mxq(x, axis, fmt="e4m3"):
    dtype, down = {"e4m3": (ml_dtypes.float8_e4m3fn, 7), "e5m2": (ml_dtypes.float8_e5m2, 14)}[fmt]
    v = np.moveaxis(np.asarray(x, np.float32).astype(ml_dtypes.bfloat16).astype(np.float64), axis, -1)
    blocks = v.reshape(v.shape[:-1] + (-1, 32))
    amax = np.abs(blocks).max(-1, keepdims=True)
    byte = np.maximum(np.where(amax > 0, np.frexp(amax)[1] - 1 + 127, 0) - down, 1)
    scale = np.exp2(byte - 127.0)
    codes = (blocks / scale).astype(np.float32).astype(dtype).astype(np.float64)
    return np.moveaxis((codes * scale).reshape(v.shape), -1, axis)


WIDE = False


def mx_kscale(k):
    if not WIDE:
        return np.ones(k)
    levels = np.array([10, -10, 5, -5, 0])
    a = np.random.permutation(np.resize(levels, k // 512 * 4)).reshape(k // 512, 4)
    idx = np.arange(k)
    return np.exp2(a[idx // 512, idx % 128 // 32])


BF16 = ml_dtypes.bfloat16


def bf(x):
    return np.asarray(x, np.float32).astype(BF16)


def f64(x):
    return np.asarray(x).astype(np.float64)


B, N, D, BD = 4, 1024, 512, 512


def setup_inputs():
    s, u = mx_kscale(D), mx_kscale(D)
    t = mx_kscale(BD)
    return {
        "keys": bf(np.random.standard_normal((B, N, D)) * s),
        "values": bf(np.random.standard_normal((B, N, D)) * u),
        "Wbk": bf(np.random.standard_normal((BD, D)) / np.sqrt(D) / s[None, :]),
        "bbk": bf(np.random.standard_normal(BD) * 0.1),
        "Wbv": bf(np.random.standard_normal((BD, D)) / np.sqrt(D) / u[None, :] * t[:, None]),
        "bbv": bf(np.random.standard_normal(BD) * 0.1 * t),
        "Wbc": bf(np.random.standard_normal((D, BD)) / np.sqrt(BD) / t[None, :]),
        "bbc": bf(np.random.standard_normal(D) * 0.1),
    }


def reference(keys, values, Wbk, bbk, Wbv, bbv, Wbc, bbc):
    k = (mxq(f64(keys), 2, "e4m3") @ mxq(f64(Wbk), 1, "e4m3").T) + f64(bbk)
    v = (mxq(f64(values), 2, "e4m3") @ mxq(f64(Wbv), 1, "e4m3").T) + f64(bbv)
    return (mxq(k * v, 2, "e4m3") @ mxq(f64(Wbc), 1, "e4m3").T) + f64(bbc)

@@ -1,0 +1,250 @@
+from contextlib import ExitStack
+
+import concourse.mybir as mybir
+from concourse.masks import make_identity
+
+F32 = mybir.dt.float32
+BF16 = mybir.dt.bfloat16
+U32 = mybir.dt.uint32
+U8 = mybir.dt.uint8
+FP8X4 = mybir.dt.float8_e4m3fn_x4
+ADD = mybir.AluOpType.add
+MULT = mybir.AluOpType.mult
+IDENTITY = mybir.ActivationFunctionType.Identity
+
+P = 128
+PACK = 4
+WIDTH = P * PACK
+BLOCK = 512
+TILES = BLOCK // P
+TOKENS = 4 * 1024
+CHUNKS = TOKENS // BLOCK
+VECTOR_REGROUPS = 64
+
+FLOPS = 3 * 2 * TOKENS * WIDTH * WIDTH
+
+HALVES = "r (i u q) -> r i u q"
+PAIRS = "r (i q u) -> r i u q"
+
+
+def tile_learnedbindingmemory_pa_t_kernel(
+    tc, keys, values, Wbk, bbk, Wbv, bbv, Wbc, bbc, out
+):
+    nc = tc.nc
+    key_rows = keys.flatten_outer_dims()
+    value_rows = values.flatten_outer_dims()
+    out_rows = out.flatten_outer_dims()
+
+    with ExitStack() as ctx:
+        ctx.enter_context(tc.manual_schedule())
+        fixed = ctx.enter_context(tc.tile_pool(name="fixed", bufs=1))
+        ring = ctx.enter_context(tc.tile_pool(name="ring", bufs=2))
+        psum = ctx.enter_context(tc.psum_pool(name="psum", bufs=2))
+
+        raw = {}
+        turned = {}
+        grouped = {}
+        codes = {}
+        scales = {}
+        projected = {}
+        planes = {}
+        combined = {}
+
+        def load(block, rows, view):
+            raw[block] = fixed.tile([P, TILES * WIDTH], BF16, name="raw_%s_%s" % block)
+            nc.sync.dma_start(
+                out=raw[block][:].rearrange("r (i d) -> r i d", i=TILES),
+                in_=rows.rearrange(view, i=TILES),
+            )
+
+        def chunk_of(rows, c):
+            return rows[c * BLOCK : (c + 1) * BLOCK, :]
+
+        NEIGHBOURS = "(r i) d -> r i d"
+        STRIPES = "(i r) d -> r i d"
+
+        bias_k16 = fixed.tile([P, PACK], BF16)
+        bias_v16 = fixed.tile([P, PACK], BF16)
+        bias_row = fixed.tile([P, WIDTH], BF16)
+        ones = fixed.tile([P, P], BF16)
+        nc.vector.memset(bias_row[:], 0.0)
+        nc.vector.memset(ones[:], 1.0)
+        nc.scalar.dma_start(out=bias_k16[:], in_=bbk.rearrange("(r t) -> r t", t=PACK))
+        nc.scalar.dma_start(out=bias_v16[:], in_=bbv.rearrange("(r t) -> r t", t=PACK))
+        nc.scalar.dma_start(out=bias_row[0:1, :], in_=bbc.unsqueeze(0))
+
+        load(("wk", 0), Wbk, NEIGHBOURS)
+        load(("k", 0), chunk_of(key_rows, 0), NEIGHBOURS)
+        load(("wv", 0), Wbv, NEIGHBOURS)
+        load(("v", 0), chunk_of(value_rows, 0), NEIGHBOURS)
+        load(("wc", 0), Wbc, STRIPES)
+        for c in range(1, CHUNKS):
+            load(("k", c), chunk_of(key_rows, c), NEIGHBOURS)
+            load(("v", c), chunk_of(value_rows, c), NEIGHBOURS)
+
+        identity = fixed.tile([P, P], F32)
+        make_identity(nc, identity[:])
+
+        bias_k = fixed.tile([P, PACK], F32)
+        bias_v = fixed.tile([P, PACK], F32)
+        nc.scalar.activation(out=bias_k[:], in_=bias_k16[:], func=IDENTITY)
+        nc.scalar.activation(out=bias_v[:], in_=bias_v16[:], func=IDENTITY)
+
+        def transpose(block, half, word_order=HALVES):
+            words = raw[block][:].bitcast(F32).rearrange(word_order, i=TILES, u=2)
+            bank = psum.tile([P, 2, 2, P], F32, name="turned", tag="turned")
+            for j in range(2):
+                for u in range(2):
+                    nc.tensor.transpose(bank[:, j, u, :], words[:, 2 * half + j, u, :], identity[:])
+            turned[(block, half)] = bank
+
+        def gather(copy, block, half):
+            if half == 0:
+                grouped[block] = ring.tile(
+                    [P, BLOCK * PACK], BF16, name="grouped", tag="grouped", bufs=4, align_bytes=64
+                )
+            pairs = grouped[block][:].bitcast(F32).rearrange("q (i n u) -> q i n u", i=TILES, u=2)
+            copy(
+                out=pairs[:, 2 * half : 2 * half + 2],
+                in_=turned[(block, half)][:].rearrange("q j u n -> q j n u"),
+            )
+
+        def quantise(block, pool, values_in):
+            kind = block[0]
+            codes[block] = pool.tile(
+                [P, BLOCK], U32, name="codes_%s_%s" % block, tag="codes_%s" % kind, align_bytes=64
+            )
+            scales[block] = pool.tile(
+                [P, BLOCK], U8, name="scales_%s_%s" % block, tag="scales_%s" % kind, align_bytes=64
+            )
+            nc.vector.quantize_mx(
+                out=codes[block][:].bitcast(FP8X4), scales=scales[block][:], in_=values_in[:]
+            )
+
+        def prepare_at_start(block, pool, word_order=HALVES):
+            transpose(block, 0, word_order)
+            transpose(block, 1, word_order)
+            gather(nc.scalar.copy, block, 0)
+            gather(nc.vector.tensor_copy, block, 1)
+            quantise(block, pool, grouped[block])
+
+        def project(stream, c, t):
+            weight = ("w" + stream, 0)
+            features = slice(t * P, (t + 1) * P)
+            bank = psum.tile([P, BLOCK], F32, name="projected", tag="projected_%s" % stream)
+            nc.tensor.matmul_mx(
+                out=bank[:],
+                lhsT=codes[weight][:, features].bitcast(FP8X4),
+                lhsT_scale=scales[weight][:, features],
+                rhs=codes[(stream, c)][:].bitcast(FP8X4),
+                rhs_scale=scales[(stream, c)][:],
+                start=True,
+                stop=True,
+            )
+            projected[(stream, c, t)] = bank
+
+        def bind(c, t):
+            if t == 0:
+                planes[c] = ring.tile([P, PACK, BLOCK], BF16, name="planes", tag="planes")
+            k_biased = ring.tile([P, BLOCK], F32, name="k_biased", tag="k_biased", bufs=4)
+            nc.scalar.activation(
+                out=k_biased[:], in_=projected[("k", c, t)][:], func=IDENTITY,
+                bias=bias_k[:, t : t + 1], scale=1.0,
+            )
+            nc.vector.scalar_tensor_tensor(
+                out=planes[c][:, t, :], in0=projected[("v", c, t)][:], scalar=bias_v[:, t : t + 1],
+                in1=k_biased[:], op0=ADD, op1=MULT,
+            )
+
+        def regroup(copy, c, first, last):
+            by_token = grouped[("p", c)][:].rearrange("r (n t) -> r n t", t=PACK)
+            copy(
+                out=by_token[:, first:last, :].rearrange("r (m s) t -> r m t s", s=4),
+                in_=planes[c][:, :, first:last].rearrange("r t (m s) -> r m t s", s=4),
+            )
+
+        def combine(c, i):
+            tokens = slice(i * P, (i + 1) * P)
+            bank = psum.tile([P, WIDTH], F32, name="combined", tag="combined")
+            nc.tensor.matmul_mx(
+                out=bank[:],
+                lhsT=codes[("p", c)][:, tokens].bitcast(FP8X4),
+                lhsT_scale=scales[("p", c)][:, tokens],
+                rhs=codes[("wc", 0)][:].bitcast(FP8X4),
+                rhs_scale=scales[("wc", 0)][:],
+                start=True,
+                stop=True,
+            )
+            combined[(c, i)] = bank
+
+        def finish(c, i):
+            result = ring.tile([P, WIDTH], F32, name="result", tag="result", bufs=6)
+            nc.vector.tensor_tensor(out=result[:], in0=combined[(c, i)][:], in1=bias_c[:], op=ADD)
+            nc.sync.dma_start(
+                out=chunk_of(out_rows, c).rearrange(NEIGHBOURS, i=TILES)[:, i, :], in_=result[:]
+            )
+
+        prepare_at_start(("wk", 0), fixed)
+        prepare_at_start(("k", 0), ring)
+        prepare_at_start(("wv", 0), fixed)
+        prepare_at_start(("v", 0), ring)
+
+        spread = psum.tile([P, WIDTH], F32, name="spread", tag="combined")
+        nc.tensor.matmul(out=spread[:], lhsT=ones[:], rhs=bias_row[:], start=True, stop=True)
+        bias_c = fixed.tile([P, WIDTH], F32)
+        nc.vector.tensor_copy(out=bias_c[:], in_=spread[:])
+
+        prepare_at_start(("wc", 0), fixed, PAIRS)
+        for stream in ("k", "v"):
+            project(stream, 0, 0)
+            project(stream, 0, 1)
+        transpose(("k", 1), 0)
+        transpose(("k", 1), 1)
+
+        live = range(CHUNKS)
+        for a in range(CHUNKS + 1):
+            before, after = a - 1, a + 1
+            if before in live:
+                quantise(("p", before), ring, grouped[("p", before)])
+            if a in live:
+                bind(a, 0)
+                bind(a, 1)
+                for stream in ("k", "v"):
+                    project(stream, a, 2)
+                    project(stream, a, 3)
+                bind(a, 2)
+                bind(a, 3)
+                grouped[("p", a)] = ring.tile(
+                    [P, BLOCK * PACK], BF16, name="grouped_p", tag="grouped_p", align_bytes=64
+                )
+                regroup(nc.vector.tensor_copy, a, 0, VECTOR_REGROUPS)
+            if before in live:
+                combine(before, 0)
+                combine(before, 1)
+                finish(before, 0)
+                finish(before, 1)
+            if after in live:
+                gather(nc.scalar.copy, ("k", after), 0)
+                gather(nc.scalar.copy, ("k", after), 1)
+                quantise(("k", after), ring, grouped[("k", after)])
+                transpose(("v", after), 0)
+                transpose(("v", after), 1)
+            if before in live:
+                combine(before, 2)
+                combine(before, 3)
+                finish(before, 2)
+            if after in live:
+                gather(nc.scalar.copy, ("v", after), 0)
+                gather(nc.scalar.copy, ("v", after), 1)
+                quantise(("v", after), ring, grouped[("v", after)])
+            if before in live:
+                finish(before, 3)
+            if after + 1 in live:
+                transpose(("k", after + 1), 0)
+                transpose(("k", after + 1), 1)
+            if after in live:
+                for stream in ("k", "v"):
+                    project(stream, after, 0)
+                    project(stream, after, 1)
+            if a in live:
+                regroup(nc.scalar.copy, a, VECTOR_REGROUPS, BLOCK)

@@ -69,16 +69,18 @@ def tile_learnedbindingmemory_pa_t_kernel(
         ones = fixed.tile([P, P], BF16)
         nc.vector.memset(bias_row[:], 0.0)
         nc.vector.memset(ones[:], 1.0)
+        nc.scalar.dma_start(out=bias_row[0:1, :], in_=bbc.unsqueeze(0))
         nc.scalar.dma_start(out=bias_k16[:], in_=bbk.rearrange("(r t) -> r t", t=PACK))
         nc.scalar.dma_start(out=bias_v16[:], in_=bbv.rearrange("(r t) -> r t", t=PACK))
-        nc.scalar.dma_start(out=bias_row[0:1, :], in_=bbc.unsqueeze(0))
 
         load(("wk", 0), Wbk, NEIGHBOURS)
         load(("k", 0), chunk_of(key_rows, 0), NEIGHBOURS)
         load(("wv", 0), Wbv, NEIGHBOURS)
         load(("v", 0), chunk_of(value_rows, 0), NEIGHBOURS)
+        load(("k", 1), chunk_of(key_rows, 1), NEIGHBOURS)
+        load(("v", 1), chunk_of(value_rows, 1), NEIGHBOURS)
         load(("wc", 0), Wbc, STRIPES)
-        for c in range(1, CHUNKS):
+        for c in range(2, CHUNKS):
             load(("k", c), chunk_of(key_rows, c), NEIGHBOURS)
             load(("v", c), chunk_of(value_rows, c), NEIGHBOURS)
 
@@ -90,26 +92,29 @@ def tile_learnedbindingmemory_pa_t_kernel(
         nc.scalar.activation(out=bias_k[:], in_=bias_k16[:], func=IDENTITY)
         nc.scalar.activation(out=bias_v[:], in_=bias_v16[:], func=IDENTITY)
 
-        def transpose(block, half, word_order=HALVES):
+        def transpose(block, bank_tag="turned", word_order=HALVES):
             words = raw[block][:].bitcast(F32).rearrange(word_order, i=TILES, u=2)
-            bank = psum.tile([P, 2, 2, P], F32, name="turned", tag="turned")
-            for j in range(2):
-                for u in range(2):
-                    nc.tensor.transpose(bank[:, j, u, :], words[:, 2 * half + j, u, :], identity[:])
-            turned[(block, half)] = bank
+            for half in range(2):
+                bank = psum.tile([P, 2, 2, P], F32, name="turned", tag=bank_tag)
+                for j in range(2):
+                    for u in range(2):
+                        nc.tensor.transpose(
+                            bank[:, j, u, :], words[:, 2 * half + j, u, :], identity[:]
+                        )
+                turned[(block, half)] = bank
 
-        def gather(copy, block, half):
-            if half == 0:
-                grouped[block] = ring.tile(
-                    [P, BLOCK * PACK], BF16, name="grouped", tag="grouped", bufs=4, align_bytes=64
-                )
-            pairs = grouped[block][:].bitcast(F32).rearrange("q (i n u) -> q i n u", i=TILES, u=2)
-            copy(
-                out=pairs[:, 2 * half : 2 * half + 2],
-                in_=turned[(block, half)][:].rearrange("q j u n -> q j n u"),
+        def gather(block, copies):
+            grouped[block] = ring.tile(
+                [P, BLOCK * PACK], BF16, name="grouped", tag="grouped", bufs=4, align_bytes=64
             )
+            pairs = grouped[block][:].bitcast(F32).rearrange("q (i n u) -> q i n u", i=TILES, u=2)
+            for half in range(2):
+                copies[half](
+                    out=pairs[:, 2 * half : 2 * half + 2],
+                    in_=turned[(block, half)][:].rearrange("q j u n -> q j n u"),
+                )
 
-        def quantise(block, pool, values_in):
+        def packed_tiles(block, pool):
             kind = block[0]
             codes[block] = pool.tile(
                 [P, BLOCK], U32, name="codes_%s_%s" % block, tag="codes_%s" % kind, align_bytes=64
@@ -117,16 +122,21 @@ def tile_learnedbindingmemory_pa_t_kernel(
             scales[block] = pool.tile(
                 [P, BLOCK], U8, name="scales_%s_%s" % block, tag="scales_%s" % kind, align_bytes=64
             )
+
+        def quantise(block, pool):
+            packed_tiles(block, pool)
             nc.vector.quantize_mx(
-                out=codes[block][:].bitcast(FP8X4), scales=scales[block][:], in_=values_in[:]
+                out=codes[block][:].bitcast(FP8X4), scales=scales[block][:], in_=grouped[block][:]
             )
 
-        def prepare_at_start(block, pool, word_order=HALVES):
-            transpose(block, 0, word_order)
-            transpose(block, 1, word_order)
-            gather(nc.scalar.copy, block, 0)
-            gather(nc.vector.tensor_copy, block, 1)
-            quantise(block, pool, grouped[block])
+        BY_SCALAR = (nc.scalar.copy, nc.scalar.copy)
+        BY_VECTOR = (nc.vector.tensor_copy, nc.vector.tensor_copy)
+        BY_BOTH = (nc.scalar.copy, nc.vector.tensor_copy)
+
+        def prepare(block, pool, bank_tag, copies, word_order=HALVES):
+            transpose(block, bank_tag, word_order)
+            gather(block, copies)
+            quantise(block, pool)
 
         def project(stream, c, t):
             weight = ("w" + stream, 0)
@@ -143,9 +153,14 @@ def tile_learnedbindingmemory_pa_t_kernel(
             )
             projected[(stream, c, t)] = bank
 
+        def project_pair(c, first):
+            for stream in ("k", "v"):
+                project(stream, c, first)
+                project(stream, c, first + 1)
+
         def bind(c, t):
             if t == 0:
-                planes[c] = ring.tile([P, PACK, BLOCK], BF16, name="planes", tag="planes")
+                planes[c] = ring.tile([P, PACK, BLOCK], BF16, name="planes", tag="planes", bufs=3)
             k_biased = ring.tile([P, BLOCK], F32, name="k_biased", tag="k_biased", bufs=4)
             nc.scalar.activation(
                 out=k_biased[:], in_=projected[("k", c, t)][:], func=IDENTITY,
@@ -161,6 +176,25 @@ def tile_learnedbindingmemory_pa_t_kernel(
             copy(
                 out=by_token[:, first:last, :].rearrange("r (m s) t -> r m t s", s=4),
                 in_=planes[c][:, :, first:last].rearrange("r t (m s) -> r m t s", s=4),
+            )
+
+        def quantise_product(c, i):
+            product = ("p", c)
+            if i == 0:
+                grouped[product] = ring.tile(
+                    [P, BLOCK * PACK], BF16, name="grouped_p", tag="grouped_p", align_bytes=64
+                )
+                packed_tiles(product, ring)
+            first, last = i * P, (i + 1) * P
+            if i < TILES - 1:
+                regroup(nc.scalar.copy, c, first, last)
+            else:
+                regroup(nc.scalar.copy, c, first, last - VECTOR_REGROUPS)
+                regroup(nc.vector.tensor_copy, c, last - VECTOR_REGROUPS, last)
+            nc.vector.quantize_mx(
+                out=codes[product][:, first:last].bitcast(FP8X4),
+                scales=scales[product][:, first:last],
+                in_=grouped[product][:, first * PACK : last * PACK],
             )
 
         def combine(c, i):
@@ -184,67 +218,59 @@ def tile_learnedbindingmemory_pa_t_kernel(
                 out=chunk_of(out_rows, c).rearrange(NEIGHBOURS, i=TILES)[:, i, :], in_=result[:]
             )
 
-        prepare_at_start(("wk", 0), fixed)
-        prepare_at_start(("k", 0), ring)
-        prepare_at_start(("wv", 0), fixed)
-        prepare_at_start(("v", 0), ring)
-
         spread = psum.tile([P, WIDTH], F32, name="spread", tag="combined")
         nc.tensor.matmul(out=spread[:], lhsT=ones[:], rhs=bias_row[:], start=True, stop=True)
         bias_c = fixed.tile([P, WIDTH], F32)
         nc.vector.tensor_copy(out=bias_c[:], in_=spread[:])
 
-        prepare_at_start(("wc", 0), fixed, PAIRS)
-        for stream in ("k", "v"):
-            project(stream, 0, 0)
-            project(stream, 0, 1)
-        transpose(("k", 1), 0)
-        transpose(("k", 1), 1)
+        prepare(("wk", 0), fixed, "projected_k", BY_BOTH)
+        prepare(("k", 0), ring, "turned", BY_BOTH)
+        prepare(("wv", 0), fixed, "projected_v", BY_BOTH)
+        prepare(("v", 0), ring, "combined", BY_BOTH)
+        transpose(("k", 1))
+        project_pair(0, 0)
+        gather(("k", 1), BY_SCALAR)
+        transpose(("v", 1))
 
         live = range(CHUNKS)
-        for a in range(CHUNKS + 1):
-            before, after = a - 1, a + 1
-            if before in live:
-                quantise(("p", before), ring, grouped[("p", before)])
+        for a in range(CHUNKS + 2):
             if a in live:
                 bind(a, 0)
                 bind(a, 1)
-                for stream in ("k", "v"):
-                    project(stream, a, 2)
-                    project(stream, a, 3)
+            if a - 2 in live:
+                combine(a - 2, 2)
+                combine(a - 2, 3)
+            if a in live:
+                project_pair(a, 2)
+            if a - 1 in live:
+                quantise_product(a - 1, 0)
+            if a + 1 in live:
+                quantise(("k", a + 1), ring)
+            if a - 1 in live:
+                quantise_product(a - 1, 1)
+            if a - 2 in live:
+                finish(a - 2, 2)
+                finish(a - 2, 3)
+            if a + 1 in live:
+                gather(("v", a + 1), BY_SCALAR)
+                quantise(("v", a + 1), ring)
+            if a + 2 in live:
+                transpose(("k", a + 2))
+            if a - 1 in live:
+                combine(a - 1, 0)
+                combine(a - 1, 1)
+            if a in live:
                 bind(a, 2)
                 bind(a, 3)
-                grouped[("p", a)] = ring.tile(
-                    [P, BLOCK * PACK], BF16, name="grouped_p", tag="grouped_p", align_bytes=64
-                )
-                regroup(nc.vector.tensor_copy, a, 0, VECTOR_REGROUPS)
-            if before in live:
-                combine(before, 0)
-                combine(before, 1)
-                finish(before, 0)
-                finish(before, 1)
-            if after in live:
-                gather(nc.scalar.copy, ("k", after), 0)
-                gather(nc.scalar.copy, ("k", after), 1)
-                quantise(("k", after), ring, grouped[("k", after)])
-                transpose(("v", after), 0)
-                transpose(("v", after), 1)
-            if before in live:
-                combine(before, 2)
-                combine(before, 3)
-                finish(before, 2)
-            if after in live:
-                gather(nc.scalar.copy, ("v", after), 0)
-                gather(nc.scalar.copy, ("v", after), 1)
-                quantise(("v", after), ring, grouped[("v", after)])
-            if before in live:
-                finish(before, 3)
-            if after + 1 in live:
-                transpose(("k", after + 1), 0)
-                transpose(("k", after + 1), 1)
-            if after in live:
-                for stream in ("k", "v"):
-                    project(stream, after, 0)
-                    project(stream, after, 1)
-            if a in live:
-                regroup(nc.scalar.copy, a, VECTOR_REGROUPS, BLOCK)
+            if a + 1 in live:
+                project_pair(a + 1, 0)
+            if a == 0:
+                prepare(("wc", 0), fixed, "combined", BY_VECTOR, PAIRS)
+            if a - 1 in live:
+                quantise_product(a - 1, 2)
+                quantise_product(a - 1, 3)
+                finish(a - 1, 0)
+                finish(a - 1, 1)
+            if a + 2 in live:
+                gather(("k", a + 2), BY_SCALAR)
+                transpose(("v", a + 2))

@@ -69,9 +69,9 @@ def tile_learnedbindingmemory_pa_t_kernel(
         ones = fixed.tile([P, P], BF16)
         nc.vector.memset(bias_row[:], 0.0)
         nc.vector.memset(ones[:], 1.0)
-        nc.scalar.dma_start(out=bias_row[0:1, :], in_=bbc.unsqueeze(0))
         nc.scalar.dma_start(out=bias_k16[:], in_=bbk.rearrange("(r t) -> r t", t=PACK))
         nc.scalar.dma_start(out=bias_v16[:], in_=bbv.rearrange("(r t) -> r t", t=PACK))
+        nc.scalar.dma_start(out=bias_row[0:1, :], in_=bbc.unsqueeze(0))
 
         load(("wk", 0), Wbk, NEIGHBOURS)
         load(("k", 0), chunk_of(key_rows, 0), NEIGHBOURS)
@@ -178,18 +178,19 @@ def tile_learnedbindingmemory_pa_t_kernel(
                 in_=planes[c][:, :, first:last].rearrange("r t (m s) -> r m t s", s=4),
             )
 
-        def quantise_product(c, i):
+        def quantise_product(c, half):
             product = ("p", c)
-            if i == 0:
+            if half == 0:
                 grouped[product] = ring.tile(
                     [P, BLOCK * PACK], BF16, name="grouped_p", tag="grouped_p", align_bytes=64
                 )
                 packed_tiles(product, ring)
-            first, last = i * P, (i + 1) * P
-            if i < TILES - 1:
-                regroup(nc.scalar.copy, c, first, last)
+            first, last = half * 2 * P, (half + 1) * 2 * P
+            regroup(nc.scalar.copy, c, first, first + P)
+            if half == 0:
+                regroup(nc.scalar.copy, c, first + P, last)
             else:
-                regroup(nc.scalar.copy, c, first, last - VECTOR_REGROUPS)
+                regroup(nc.scalar.copy, c, first + P, last - VECTOR_REGROUPS)
                 regroup(nc.vector.tensor_copy, c, last - VECTOR_REGROUPS, last)
             nc.vector.quantize_mx(
                 out=codes[product][:, first:last].bitcast(FP8X4),
@@ -218,10 +219,12 @@ def tile_learnedbindingmemory_pa_t_kernel(
                 out=chunk_of(out_rows, c).rearrange(NEIGHBOURS, i=TILES)[:, i, :], in_=result[:]
             )
 
-        spread = psum.tile([P, WIDTH], F32, name="spread", tag="combined")
-        nc.tensor.matmul(out=spread[:], lhsT=ones[:], rhs=bias_row[:], start=True, stop=True)
         bias_c = fixed.tile([P, WIDTH], F32)
-        nc.vector.tensor_copy(out=bias_c[:], in_=spread[:])
+
+        def spread_bias_c():
+            spread = psum.tile([P, WIDTH], F32, name="spread", tag="combined")
+            nc.tensor.matmul(out=spread[:], lhsT=ones[:], rhs=bias_row[:], start=True, stop=True)
+            nc.vector.tensor_copy(out=bias_c[:], in_=spread[:])
 
         prepare(("wk", 0), fixed, "projected_k", BY_BOTH)
         prepare(("k", 0), ring, "turned", BY_BOTH)
@@ -242,12 +245,10 @@ def tile_learnedbindingmemory_pa_t_kernel(
                 combine(a - 2, 3)
             if a in live:
                 project_pair(a, 2)
-            if a - 1 in live:
-                quantise_product(a - 1, 0)
             if a + 1 in live:
                 quantise(("k", a + 1), ring)
             if a - 1 in live:
-                quantise_product(a - 1, 1)
+                quantise_product(a - 1, 0)
             if a - 2 in live:
                 finish(a - 2, 2)
                 finish(a - 2, 3)
@@ -262,13 +263,13 @@ def tile_learnedbindingmemory_pa_t_kernel(
             if a in live:
                 bind(a, 2)
                 bind(a, 3)
+            if a == 0:
+                spread_bias_c()
+                prepare(("wc", 0), fixed, "combined", BY_VECTOR, PAIRS)
             if a + 1 in live:
                 project_pair(a + 1, 0)
-            if a == 0:
-                prepare(("wc", 0), fixed, "combined", BY_VECTOR, PAIRS)
             if a - 1 in live:
-                quantise_product(a - 1, 2)
-                quantise_product(a - 1, 3)
+                quantise_product(a - 1, 1)
                 finish(a - 1, 0)
                 finish(a - 1, 1)
             if a + 2 in live:

@@ -36,7 +36,6 @@ def tile_learnedbindingmemory_pa_t_kernel(
     out_rows = out.flatten_outer_dims()
 
     with ExitStack() as ctx:
-        ctx.enter_context(tc.manual_schedule())
         fixed = ctx.enter_context(tc.tile_pool(name="fixed", bufs=1))
         ring = ctx.enter_context(tc.tile_pool(name="ring", bufs=2))
         psum = ctx.enter_context(tc.psum_pool(name="psum", bufs=2))

from contextlib import ExitStack

import concourse.mybir as mybir
from concourse.masks import make_identity

F32 = mybir.dt.float32
BF16 = mybir.dt.bfloat16
U32 = mybir.dt.uint32
U8 = mybir.dt.uint8
FP8X4 = mybir.dt.float8_e4m3fn_x4
ADD = mybir.AluOpType.add
MULT = mybir.AluOpType.mult
IDENTITY = mybir.ActivationFunctionType.Identity

P = 128
PACK = 4
WIDTH = P * PACK
BLOCK = 512
TILES = BLOCK // P
TOKENS = 4 * 1024
CHUNKS = TOKENS // BLOCK
VECTOR_REGROUPS = 64

FLOPS = 3 * 2 * TOKENS * WIDTH * WIDTH

HALVES = "r (i u q) -> r i u q"
PAIRS = "r (i q u) -> r i u q"


def tile_learnedbindingmemory_pa_t_kernel(
    tc, keys, values, Wbk, bbk, Wbv, bbv, Wbc, bbc, out
):
    nc = tc.nc
    key_rows = keys.flatten_outer_dims()
    value_rows = values.flatten_outer_dims()
    out_rows = out.flatten_outer_dims()

    with ExitStack() as ctx:
        fixed = ctx.enter_context(tc.tile_pool(name="fixed", bufs=1))
        ring = ctx.enter_context(tc.tile_pool(name="ring", bufs=2))
        psum = ctx.enter_context(tc.psum_pool(name="psum", bufs=2))

        raw = {}
        turned = {}
        grouped = {}
        codes = {}
        scales = {}
        projected = {}
        planes = {}
        combined = {}

        def load(block, rows, view):
            raw[block] = fixed.tile([P, TILES * WIDTH], BF16, name="raw_%s_%s" % block)
            nc.sync.dma_start(
                out=raw[block][:].rearrange("r (i d) -> r i d", i=TILES),
                in_=rows.rearrange(view, i=TILES),
            )

        def chunk_of(rows, c):
            return rows[c * BLOCK : (c + 1) * BLOCK, :]

        NEIGHBOURS = "(r i) d -> r i d"
        STRIPES = "(i r) d -> r i d"

        bias_k16 = fixed.tile([P, PACK], BF16)
        bias_v16 = fixed.tile([P, PACK], BF16)
        bias_row = fixed.tile([P, WIDTH], BF16)
        ones = fixed.tile([P, P], BF16)
        nc.vector.memset(bias_row[:], 0.0)
        nc.vector.memset(ones[:], 1.0)
        nc.scalar.dma_start(out=bias_k16[:], in_=bbk.rearrange("(r t) -> r t", t=PACK))
        nc.scalar.dma_start(out=bias_v16[:], in_=bbv.rearrange("(r t) -> r t", t=PACK))
        nc.scalar.dma_start(out=bias_row[0:1, :], in_=bbc.unsqueeze(0))

        load(("wk", 0), Wbk, NEIGHBOURS)
        load(("k", 0), chunk_of(key_rows, 0), NEIGHBOURS)
        load(("wv", 0), Wbv, NEIGHBOURS)
        load(("v", 0), chunk_of(value_rows, 0), NEIGHBOURS)
        load(("k", 1), chunk_of(key_rows, 1), NEIGHBOURS)
        load(("v", 1), chunk_of(value_rows, 1), NEIGHBOURS)
        load(("wc", 0), Wbc, STRIPES)
        for c in range(2, CHUNKS):
            load(("k", c), chunk_of(key_rows, c), NEIGHBOURS)
            load(("v", c), chunk_of(value_rows, c), NEIGHBOURS)

        identity = fixed.tile([P, P], F32)
        make_identity(nc, identity[:])

        bias_k = fixed.tile([P, PACK], F32)
        bias_v = fixed.tile([P, PACK], F32)
        nc.scalar.activation(out=bias_k[:], in_=bias_k16[:], func=IDENTITY)
        nc.scalar.activation(out=bias_v[:], in_=bias_v16[:], func=IDENTITY)

        def transpose(block, bank_tag="turned", word_order=HALVES):
            words = raw[block][:].bitcast(F32).rearrange(word_order, i=TILES, u=2)
            for half in range(2):
                bank = psum.tile([P, 2, 2, P], F32, name="turned", tag=bank_tag)
                for j in range(2):
                    for u in range(2):
                        nc.tensor.transpose(
                            bank[:, j, u, :], words[:, 2 * half + j, u, :], identity[:]
                        )
                turned[(block, half)] = bank

        def gather(block, copies):
            grouped[block] = ring.tile(
                [P, BLOCK * PACK], BF16, name="grouped", tag="grouped", bufs=4, align_bytes=64
            )
            pairs = grouped[block][:].bitcast(F32).rearrange("q (i n u) -> q i n u", i=TILES, u=2)
            for half in range(2):
                copies[half](
                    out=pairs[:, 2 * half : 2 * half + 2],
                    in_=turned[(block, half)][:].rearrange("q j u n -> q j n u"),
                )

        def packed_tiles(block, pool):
            kind = block[0]
            codes[block] = pool.tile(
                [P, BLOCK], U32, name="codes_%s_%s" % block, tag="codes_%s" % kind, align_bytes=64
            )
            scales[block] = pool.tile(
                [P, BLOCK], U8, name="scales_%s_%s" % block, tag="scales_%s" % kind, align_bytes=64
            )

        def quantise(block, pool):
            packed_tiles(block, pool)
            nc.vector.quantize_mx(
                out=codes[block][:].bitcast(FP8X4), scales=scales[block][:], in_=grouped[block][:]
            )

        BY_SCALAR = (nc.scalar.copy, nc.scalar.copy)
        BY_VECTOR = (nc.vector.tensor_copy, nc.vector.tensor_copy)
        BY_BOTH = (nc.scalar.copy, nc.vector.tensor_copy)

        def prepare(block, pool, bank_tag, copies, word_order=HALVES):
            transpose(block, bank_tag, word_order)
            gather(block, copies)
            quantise(block, pool)

        def project(stream, c, t):
            weight = ("w" + stream, 0)
            features = slice(t * P, (t + 1) * P)
            bank = psum.tile([P, BLOCK], F32, name="projected", tag="projected_%s" % stream)
            nc.tensor.matmul_mx(
                out=bank[:],
                lhsT=codes[weight][:, features].bitcast(FP8X4),
                lhsT_scale=scales[weight][:, features],
                rhs=codes[(stream, c)][:].bitcast(FP8X4),
                rhs_scale=scales[(stream, c)][:],
                start=True,
                stop=True,
            )
            projected[(stream, c, t)] = bank

        def project_pair(c, first):
            for stream in ("k", "v"):
                project(stream, c, first)
                project(stream, c, first + 1)

        def bind(c, t):
            if t == 0:
                planes[c] = ring.tile([P, PACK, BLOCK], BF16, name="planes", tag="planes", bufs=3)
            k_biased = ring.tile([P, BLOCK], F32, name="k_biased", tag="k_biased", bufs=4)
            nc.scalar.activation(
                out=k_biased[:], in_=projected[("k", c, t)][:], func=IDENTITY,
                bias=bias_k[:, t : t + 1], scale=1.0,
            )
            nc.vector.scalar_tensor_tensor(
                out=planes[c][:, t, :], in0=projected[("v", c, t)][:], scalar=bias_v[:, t : t + 1],
                in1=k_biased[:], op0=ADD, op1=MULT,
            )

        def regroup(copy, c, first, last):
            by_token = grouped[("p", c)][:].rearrange("r (n t) -> r n t", t=PACK)
            copy(
                out=by_token[:, first:last, :].rearrange("r (m s) t -> r m t s", s=4),
                in_=planes[c][:, :, first:last].rearrange("r t (m s) -> r m t s", s=4),
            )

        def quantise_product(c, half):
            product = ("p", c)
            if half == 0:
                grouped[product] = ring.tile(
                    [P, BLOCK * PACK], BF16, name="grouped_p", tag="grouped_p", align_bytes=64
                )
                packed_tiles(product, ring)
            first, last = half * 2 * P, (half + 1) * 2 * P
            regroup(nc.scalar.copy, c, first, first + P)
            if half == 0:
                regroup(nc.scalar.copy, c, first + P, last)
            else:
                regroup(nc.scalar.copy, c, first + P, last - VECTOR_REGROUPS)
                regroup(nc.vector.tensor_copy, c, last - VECTOR_REGROUPS, last)
            nc.vector.quantize_mx(
                out=codes[product][:, first:last].bitcast(FP8X4),
                scales=scales[product][:, first:last],
                in_=grouped[product][:, first * PACK : last * PACK],
            )

        def combine(c, i):
            tokens = slice(i * P, (i + 1) * P)
            bank = psum.tile([P, WIDTH], F32, name="combined", tag="combined")
            nc.tensor.matmul_mx(
                out=bank[:],
                lhsT=codes[("p", c)][:, tokens].bitcast(FP8X4),
                lhsT_scale=scales[("p", c)][:, tokens],
                rhs=codes[("wc", 0)][:].bitcast(FP8X4),
                rhs_scale=scales[("wc", 0)][:],
                start=True,
                stop=True,
            )
            combined[(c, i)] = bank

        def finish(c, i):
            result = ring.tile([P, WIDTH], F32, name="result", tag="result", bufs=6)
            nc.vector.tensor_tensor(out=result[:], in0=combined[(c, i)][:], in1=bias_c[:], op=ADD)
            nc.sync.dma_start(
                out=chunk_of(out_rows, c).rearrange(NEIGHBOURS, i=TILES)[:, i, :], in_=result[:]
            )

        bias_c = fixed.tile([P, WIDTH], F32)

        def spread_bias_c():
            spread = psum.tile([P, WIDTH], F32, name="spread", tag="combined")
            nc.tensor.matmul(out=spread[:], lhsT=ones[:], rhs=bias_row[:], start=True, stop=True)
            nc.vector.tensor_copy(out=bias_c[:], in_=spread[:])

        prepare(("wk", 0), fixed, "projected_k", BY_BOTH)
        prepare(("k", 0), ring, "turned", BY_BOTH)
        prepare(("wv", 0), fixed, "projected_v", BY_BOTH)
        prepare(("v", 0), ring, "combined", BY_BOTH)
        transpose(("k", 1))
        project_pair(0, 0)
        gather(("k", 1), BY_SCALAR)
        transpose(("v", 1))

        live = range(CHUNKS)
        for a in range(CHUNKS + 2):
            if a in live:
                bind(a, 0)
                bind(a, 1)
            if a - 2 in live:
                combine(a - 2, 2)
                combine(a - 2, 3)
            if a in live:
                project_pair(a, 2)
            if a + 1 in live:
                quantise(("k", a + 1), ring)
            if a - 1 in live:
                quantise_product(a - 1, 0)
            if a - 2 in live:
                finish(a - 2, 2)
                finish(a - 2, 3)
            if a + 1 in live:
                gather(("v", a + 1), BY_SCALAR)
                quantise(("v", a + 1), ring)
            if a + 2 in live:
                transpose(("k", a + 2))
            if a - 1 in live:
                combine(a - 1, 0)
                combine(a - 1, 1)
            if a in live:
                bind(a, 2)
                bind(a, 3)
            if a == 0:
                spread_bias_c()
                prepare(("wc", 0), fixed, "combined", BY_VECTOR, PAIRS)
            if a + 1 in live:
                project_pair(a + 1, 0)
            if a - 1 in live:
                quantise_product(a - 1, 1)
                finish(a - 1, 0)
                finish(a - 1, 1)
            if a + 2 in live:
                gather(("k", a + 2), BY_SCALAR)
                transpose(("v", a + 2))
